import numpy as np
import ml_dtypes


def mxq(x, axis, fmt="e4m3"):
    dtype, down = {"e4m3": (ml_dtypes.float8_e4m3fn, 7), "e5m2": (ml_dtypes.float8_e5m2, 14)}[fmt]
    v = np.moveaxis(np.asarray(x, np.float32).astype(ml_dtypes.bfloat16).astype(np.float64), axis, -1)
    blocks = v.reshape(v.shape[:-1] + (-1, 32))
    amax = np.abs(blocks).max(-1, keepdims=True)
    byte = np.maximum(np.where(amax > 0, np.frexp(amax)[1] - 1 + 127, 0) - down, 1)
    scale = np.exp2(byte - 127.0)
    codes = (blocks / scale).astype(np.float32).astype(dtype).astype(np.float64)
    return np.moveaxis((codes * scale).reshape(v.shape), -1, axis)


WIDE = False


def mx_kscale(k):
    if not WIDE:
        return np.ones(k)
    levels = np.array([10, -10, 5, -5, 0])
    a = np.random.permutation(np.resize(levels, k // 512 * 4)).reshape(k // 512, 4)
    idx = np.arange(k)
    return np.exp2(a[idx // 512, idx % 128 // 32])


BF16 = ml_dtypes.bfloat16


def bf(x):
    return np.asarray(x, np.float32).astype(BF16)


def f64(x):
    return np.asarray(x).astype(np.float64)


B, T, C, DIM = 4, 1024, 512, 192
A = 3.0
VS = 3.0


def setup_inputs():
    g = A / np.sqrt(1.0 + np.arange(C))
    s = mx_kscale(T)
    f = s / s.min()
    a = np.log2(f)
    d0 = np.sqrt(2.0 * np.sum(g * g))
    R = np.sqrt((d0 + a * np.log(2.0)) ** 2 - d0 ** 2)
    q = np.random.standard_normal((B, T, C)) * g
    k = np.random.standard_normal((B, T, C)) * g
    k[:, :, -1] += R[None, :]
    v = np.random.standard_normal((B, T, C)) * VS * f[None, :, None]
    return {"q_scaled": bf(q), "k_scaled": bf(k), "v": bf(v)}


def reference(q_scaled, k_scaled, v):
    q2 = np.sum(f64(q_scaled) * f64(q_scaled), axis=-1)
    k2 = np.sum(f64(k_scaled) * f64(k_scaled), axis=-1)
    d2 = q2[:, :, None] + k2[:, None, :] - 2.0 * (f64(q_scaled) @ f64(k_scaled).transpose(0, 2, 1))
    d2 = np.maximum(d2, 0.0)
    dist = np.where(d2 > 0, np.sqrt(np.where(d2 > 0, d2, 1.0)), 0.0)
    logits = -dist
    e = np.exp(logits - logits.max(-1, keepdims=True))
    return (mxq(e, 2, "e4m3") @ mxq(f64(v), 1, "e4m3")) / e.sum(-1, keepdims=True)

@@ -1,0 +1,356 @@
+from contextlib import ExitStack
+
+import concourse.mybir as mybir
+from concourse.masks import make_identity
+
+F32 = mybir.dt.float32
+BF16 = mybir.dt.bfloat16
+U32 = mybir.dt.uint32
+U8 = mybir.dt.uint8
+FP8X4 = mybir.dt.float8_e4m3fn_x4
+ALU = mybir.AluOpType
+ACT = mybir.ActivationFunctionType
+
+B, T, C = 4, 1024, 512
+P = 128
+TILES = T // P
+ALL_TILES = B * TILES
+CHUNKS = C // P
+BANK = 512
+HALVES = T // BANK
+ALL_BANKS = ALL_TILES * HALVES
+TILES_PER_BANK = BANK // P
+PACK = 4
+PASSES = T // (P * PACK)
+PAIR = 2
+
+FLOPS = 2 * (2 * B * T * T * C)
+
+D2_FLOOR = 2.0**-116
+D2_FLOOR_OF_Q2 = 2.0**-23
+
+KEYS_AHEAD = 9
+QUERY_AHEAD = 2
+PHASE_LAG = 5
+TILES_PER_PHASE_STEP = 2
+PHASE_STEPS = TILES // TILES_PER_PHASE_STEP
+RECIPROCAL_LAG = 2
+VALUES_LAG = 5
+TRANSPOSE_LAG = 10
+QUANTISE_LAG = 11
+PV_LAG = 12
+STORE_LAG = 13
+LOAD_KEYS_AHEAD = 17
+LOAD_QUERIES_AHEAD = 10
+LOAD_VALUES_AHEAD = 8
+KEY_LOADS = 4
+FIRST_STEP = -KEYS_AHEAD
+LAST_STEP = ALL_TILES - 1 + STORE_LAG
+
+
+def tile_qkvattention_pa_t_kernel(tc, q_scaled, k_scaled, v, out):
+    nc = tc.nc
+    with ExitStack() as stack:
+        sbuf = stack.enter_context(tc.tile_pool(name="sbuf", bufs=1))
+        psum = stack.enter_context(tc.psum_pool(name="psum", bufs=1))
+        stack.enter_context(tc.manual_schedule())
+
+        identity = sbuf.tile([P, P], F32, name="identity")
+        make_identity(nc, identity[:])
+
+        q_rows, k_rows, v_rows = {}, {}, {}
+        q2, z_cap, k2, bank_start, k_t = {}, {}, {}, {}, {}
+        z_max, d2_min, dist, dist_min, row_sum, row_scale = {}, {}, {}, {}, {}, {}
+        v_grouped, v_codes, v_scales = {}, {}, {}
+        q_t, z, e, e_bank, e_grouped, e_codes, e_scales, acc = {}, {}, {}, {}, {}, {}, {}, {}
+        s_bank, t_bank = {}, {}
+
+        def is_batch(b):
+            return 0 <= b < B
+
+        def is_tile(n):
+            return 0 <= n < ALL_TILES
+
+        def is_bank(m):
+            return 0 <= m < ALL_BANKS
+
+        def transpose_bank(name):
+            return psum.tile([P, PAIR, PAIR, P], F32, name=name, tag="transposes", bufs=3)
+
+        def load_inputs(step):
+            for b in range(B):
+                if step == max(FIRST_STEP, TILES * b - LOAD_KEYS_AHEAD):
+                    k_rows[b] = sbuf.tile([P, TILES, C], BF16, name="k_rows", tag="k_rows", bufs=2)
+                    source = k_scaled[b].rearrange("(i p) c -> p i c", p=P)
+                    for part in range(KEY_LOADS):
+                        tiles = slice(part * TILES // KEY_LOADS, (part + 1) * TILES // KEY_LOADS)
+                        nc.sync.dma_start(out=k_rows[b][:, tiles, :], in_=source[:, tiles, :])
+                if step == max(FIRST_STEP, TILES * b - LOAD_QUERIES_AHEAD):
+                    q_rows[b] = sbuf.tile([P, TILES, C], BF16, name="q_rows", tag="q_rows", bufs=2)
+                    nc.sync.dma_start(out=q_rows[b][:], in_=q_scaled[b].rearrange("(i p) c -> p i c", p=P))
+                if step == max(FIRST_STEP, TILES * b - LOAD_VALUES_AHEAD):
+                    v_rows[b] = sbuf.tile([P, PASSES, PACK, C], BF16, name="v_rows", tag="v_rows", bufs=2)
+                    nc.sync.dma_start(
+                        out=v_rows[b][:].rearrange("p g (u w) c -> p (g u) (w c)", w=PAIR),
+                        in_=v[b].rearrange("(a p w) c -> p a (w c)", p=P, w=PAIR),
+                    )
+
+        def sum_of_squares(rows, total):
+            squares = sbuf.tile([P, C], BF16, name="squares", tag="squares", bufs=4)
+            nc.scalar.activation(out=squares[:], in_=rows, func=ACT.Square, accum_out=total)
+
+        def query_norm(n):
+            b, i = divmod(n, TILES)
+            if i == 0:
+                q2[b] = sbuf.tile([P, TILES], F32, name="q2", tag="q2", bufs=2)
+                z_cap[b] = sbuf.tile([P, TILES], F32, name="z_cap", tag="z_cap", bufs=2)
+            sum_of_squares(q_rows[b][:, i, :], q2[b][:, i : i + 1])
+            nc.gpsimd.tensor_scalar(
+                out=z_cap[b][:, i : i + 1],
+                in0=q2[b][:, i : i + 1],
+                scalar1=0.5 * (1.0 - D2_FLOOR_OF_Q2),
+                scalar2=-0.5 * D2_FLOOR,
+                op0=ALU.mult,
+                op1=ALU.add,
+            )
+
+        def key_norm(b, j):
+            if j == 0:
+                k2[b] = sbuf.tile([P, TILES], F32, name="k2", tag="k2", bufs=2)
+                bank_start[b] = sbuf.tile([P, TILES], F32, name="bank_start", tag="bank_start", bufs=3)
+            sum_of_squares(k_rows[b][:, j, :], k2[b][:, j : j + 1])
+            nc.gpsimd.tensor_scalar(
+                out=bank_start[b][:, j : j + 1],
+                in0=k2[b][:, j : j + 1],
+                scalar1=-0.5,
+                scalar2=0.0,
+                op0=ALU.mult,
+                op1=ALU.add,
+            )
+
+        def transpose_operand(step, number):
+            n = step + QUERY_AHEAD
+            b_k, j = divmod(step + KEYS_AHEAD, TILES)
+            if number == 0 and (is_tile(n) or is_batch(b_k)):
+                t_bank[step] = transpose_bank("t_bank")
+            side, u = divmod(number, PAIR)
+            words = slice(u * P, (u + 1) * P)
+            if side == 0 and is_tile(n):
+                b, i = divmod(n, TILES)
+                nc.tensor.transpose(
+                    out=t_bank[step][:, 0, u, :], in_=q_rows[b][:, i, :].bitcast(F32)[:, words], identity=identity[:]
+                )
+            if side == 1 and is_batch(b_k):
+                nc.tensor.transpose(
+                    out=t_bank[step][:, 1, u, :], in_=k_rows[b_k][:, j, :].bitcast(F32)[:, words], identity=identity[:]
+                )
+
+        def copy_operands(step):
+            n = step + QUERY_AHEAD
+            b_k, j = divmod(step + KEYS_AHEAD, TILES)
+            if is_tile(n):
+                q_t[n] = sbuf.tile([P, PAIR, P], F32, name="q_t", tag="q_t", bufs=4)
+                nc.vector.tensor_copy(out=q_t[n][:], in_=t_bank[step][:, 0])
+            if is_batch(b_k):
+                if j == 0:
+                    k_t[b_k] = sbuf.tile([P, PAIR, T], F32, name="k_t", tag="k_t", bufs=2)
+                nc.vector.tensor_copy(out=k_t[b_k][:, :, j * P : (j + 1) * P], in_=t_bank[step][:, 1])
+
+        def start_bank(m, r):
+            n, h = divmod(m, HALVES)
+            if r == 0:
+                s_bank[m] = psum.tile([P, BANK], F32, name="s_bank", tag="s_bank", bufs=3)
+            j = TILES_PER_BANK * h + r
+            nc.tensor.matmul(
+                out=s_bank[m][:, r * P : (r + 1) * P],
+                lhsT=bank_start[n // TILES][:, j : j + 1].to_broadcast([P, P]),
+                rhs=identity[:],
+                start=(r == 0),
+                stop=False,
+                is_transpose=True,
+            )
+
+        def score_matmul(m, c):
+            n, h = divmod(m, HALVES)
+            u, w = divmod(c, PAIR)
+            queries = q_t[n][:].bitcast(BF16).rearrange("p u (t w) -> p u t w", w=PAIR)
+            keys = k_t[n // TILES][:].bitcast(BF16).rearrange("p u (s w) -> p u s w", w=PAIR)
+            nc.tensor.matmul(
+                out=s_bank[m][:],
+                lhsT=queries[:, u, :, w],
+                rhs=keys[:, u, h * BANK : (h + 1) * BANK, w],
+                start=False,
+                stop=(c == CHUNKS - 1),
+            )
+
+        def cap_and_maximum(m):
+            n, h = divmod(m, HALVES)
+            b, i = divmod(n, TILES)
+            if i == 0 and h == 0:
+                z_max[b] = sbuf.tile([P, TILES, HALVES], F32, name="z_max", tag="z_max", bufs=2)
+            if h == 0:
+                z[n] = sbuf.tile([P, T], F32, name="z", tag="z", bufs=7)
+            nc.vector.tensor_scalar(
+                out=z[n][:, h * BANK : (h + 1) * BANK],
+                in0=s_bank[m][:],
+                scalar1=z_cap[b][:, i : i + 1],
+                scalar2=None,
+                op0=ALU.min,
+                op1=ALU.max,
+                accum_out=z_max[b][:, i, h : h + 1],
+            )
+
+        def nearest_keys(b):
+            d2_min[b] = sbuf.tile([P, TILES], F32, name="d2_min", tag="d2_min", bufs=2)
+            nc.vector.tensor_reduce(out=d2_min[b][:], in_=z_max[b][:], axis=mybir.AxisListType.X, op=ALU.max)
+            nc.vector.scalar_tensor_tensor(
+                out=d2_min[b][:], in0=d2_min[b][:], scalar=-2.0, in1=q2[b][:], op0=ALU.mult, op1=ALU.add
+            )
+
+        def roots(b, first_tile):
+            if first_tile == 0:
+                dist[b] = sbuf.tile([P, TILES, T], F32, name="dist", tag="dist", bufs=1)
+            for i in range(first_tile, first_tile + TILES_PER_PHASE_STEP):
+                nc.scalar.activation(
+                    out=dist[b][:, i, :], in_=z[TILES * b + i][:], func=ACT.Sqrt, scale=-2.0, bias=q2[b][:, i : i + 1]
+                )
+            if first_tile + TILES_PER_PHASE_STEP == TILES:
+                dist_min[b] = sbuf.tile([P, TILES], F32, name="dist_min", tag="dist_min", bufs=2)
+                nc.scalar.activation(out=dist_min[b][:], in_=d2_min[b][:], func=ACT.Sqrt)
+
+        def exps(b, first_tile):
+            if first_tile == 0:
+                row_sum[b] = sbuf.tile([P, TILES], F32, name="row_sum", tag="row_sum", bufs=2)
+            for i in range(first_tile, first_tile + TILES_PER_PHASE_STEP):
+                n = TILES * b + i
+                e[n] = sbuf.tile([P, T], BF16, name="e", tag="e", bufs=7)
+                nc.scalar.activation(
+                    out=e[n][:],
+                    in_=dist[b][:, i, :],
+                    func=ACT.Exp,
+                    scale=-1.0,
+                    bias=dist_min[b][:, i : i + 1],
+                    accum_out=row_sum[b][:, i : i + 1],
+                )
+
+        def reciprocals(b, first_tile):
+            if first_tile == 0:
+                row_scale[b] = sbuf.tile([P, TILES], F32, name="row_scale", tag="row_scale", bufs=2)
+            tiles = slice(first_tile, first_tile + TILES_PER_PHASE_STEP)
+            nc.vector.reciprocal(out=row_scale[b][:, tiles], in_=row_sum[b][:, tiles])
+
+        def regroup_values(b, g):
+            if g == 0:
+                v_codes[b] = sbuf.tile([P, PASSES, C], U32, name="v_codes", tag="v_codes", bufs=2, align_bytes=64)
+                v_scales[b] = sbuf.tile([P, PASSES, C], U8, name="v_scales", tag="v_scales", bufs=2, align_bytes=64)
+            v_grouped[b, g] = sbuf.tile([P, C, PACK], BF16, name="v_grouped", tag="v_grouped", bufs=2, align_bytes=64)
+            nc.gpsimd.tensor_scalar(
+                out=v_grouped[b, g][:].rearrange("p (c r) j -> p c j r", r=4),
+                in0=v_rows[b][:, g].rearrange("p j (c r) -> p c j r", r=4),
+                scalar1=1.0,
+                scalar2=0.0,
+                op0=ALU.mult,
+                op1=ALU.add,
+            )
+
+        def quantise_values(b, g):
+            nc.vector.quantize_mx(
+                out=v_codes[b][:, g, :].bitcast(FP8X4),
+                scales=v_scales[b][:, g, :],
+                in_=v_grouped[b, g][:].rearrange("p c j -> p (c j)"),
+            )
+
+        def transpose_e(n, a):
+            if a == 0:
+                e_bank[n] = transpose_bank("e_bank")
+            g, u = divmod(a, PAIR)
+            nc.tensor.transpose(
+                out=e_bank[n][:, g, u, :], in_=e[n][:].bitcast(F32)[:, a * P : (a + 1) * P], identity=identity[:]
+            )
+
+        def copy_e(n):
+            e_grouped[n] = sbuf.tile([P, PASSES, P, PACK], BF16, name="e_grouped", tag="e_grouped", bufs=3, align_bytes=64)
+            nc.vector.tensor_copy(out=e_grouped[n][:].bitcast(F32), in_=e_bank[n][:].rearrange("p g u t -> p g t u"))
+
+        def quantise_e(n):
+            e_codes[n] = sbuf.tile([P, PASSES, P], U32, name="e_codes", tag="e_codes", bufs=3, align_bytes=64)
+            e_scales[n] = sbuf.tile([P, PASSES, P], U8, name="e_scales", tag="e_scales", bufs=3, align_bytes=64)
+            nc.vector.quantize_mx(
+                out=e_codes[n][:].rearrange("p g t -> p (g t)").bitcast(FP8X4),
+                scales=e_scales[n][:].rearrange("p g t -> p (g t)"),
+                in_=e_grouped[n][:].rearrange("p g t j -> p (g t j)"),
+            )
+
+        def multiply_with_values(n):
+            b = n // TILES
+            acc[n] = psum.tile([P, C], F32, name="acc", tag="acc", bufs=2)
+            for g in range(PASSES):
+                nc.tensor.matmul_mx(
+                    out=acc[n][:],
+                    lhsT=e_codes[n][:, g, :].bitcast(FP8X4),
+                    lhsT_scale=e_scales[n][:, g, :],
+                    rhs=v_codes[b][:, g, :].bitcast(FP8X4),
+                    rhs_scale=v_scales[b][:, g, :],
+                    start=(g == 0),
+                    stop=(g == PASSES - 1),
+                )
+
+        def scale_and_store(n):
+            b, i = divmod(n, TILES)
+            out_rows = sbuf.tile([P, C], F32, name="out_rows", tag="out_rows", bufs=4)
+            nc.vector.tensor_scalar(
+                out=out_rows[:], in0=acc[n][:], scalar1=row_scale[b][:, i : i + 1], scalar2=None, op0=ALU.mult
+            )
+            nc.sync.dma_start(out=out[b, i * P : (i + 1) * P, :], in_=out_rows[:])
+
+        for step in range(FIRST_STEP, LAST_STEP + 1):
+            load_inputs(step)
+            phase_batch, phase_step = divmod(step - PHASE_LAG, TILES)
+            if is_batch(phase_batch) and phase_step == PHASE_STEPS - 1:
+                nearest_keys(phase_batch)
+            b, j = divmod(step + KEYS_AHEAD, TILES)
+            if is_batch(b):
+                key_norm(b, j)
+            if is_tile(step + QUERY_AHEAD):
+                query_norm(step + QUERY_AHEAD)
+
+            for h in range(HALVES):
+                m = HALVES * step + h
+                for c in range(CHUNKS):
+                    if is_bank(m):
+                        score_matmul(m, c)
+                    if is_bank(m + 1):
+                        start_bank(m + 1, c)
+                    if h == 0:
+                        transpose_operand(step, c)
+                    elif is_tile(step - TRANSPOSE_LAG):
+                        transpose_e(step - TRANSPOSE_LAG, c)
+                if is_bank(m):
+                    cap_and_maximum(m)
+                if h == 0:
+                    copy_operands(step)
+                elif is_tile(step - TRANSPOSE_LAG):
+                    copy_e(step - TRANSPOSE_LAG)
+
+            if is_batch(phase_batch):
+                if phase_step < PHASE_STEPS:
+                    roots(phase_batch, phase_step * TILES_PER_PHASE_STEP)
+                else:
+                    exps(phase_batch, (phase_step - PHASE_STEPS) * TILES_PER_PHASE_STEP)
+            b, pair = divmod(step - PHASE_LAG - PHASE_STEPS - RECIPROCAL_LAG, TILES)
+            if is_batch(b) and pair < PHASE_STEPS:
+                reciprocals(b, pair * TILES_PER_PHASE_STEP)
+
+            if is_tile(step - QUANTISE_LAG):
+                quantise_e(step - QUANTISE_LAG)
+            if is_tile(step - PV_LAG):
+                multiply_with_values(step - PV_LAG)
+            if is_tile(step - STORE_LAG):
+                scale_and_store(step - STORE_LAG)
+
+            b, part = divmod(step - VALUES_LAG, TILES)
+            if is_batch(b) and part < 2 * PASSES:
+                if part % 2 == 0:
+                    regroup_values(b, part // 2)
+                else:
+                    quantise_values(b, part // 2)

@@ -25,27 +25,92 @@ PASSES = T // (P * PACK)
 PAIR = 2
 
 FLOPS = 2 * (2 * B * T * T * C)
-
 D2_FLOOR = 2.0**-116
 D2_FLOOR_OF_Q2 = 2.0**-23
 
-KEYS_AHEAD = 9
+FIRST_STEP = -3
+GROUP = 8
+ROOT_LAG = 2
+SCALAR_LOAD = 5
+SQUARES_AHEAD = 8
 QUERY_AHEAD = 2
-PHASE_LAG = 5
-TILES_PER_PHASE_STEP = 2
-PHASE_STEPS = TILES // TILES_PER_PHASE_STEP
-RECIPROCAL_LAG = 2
-VALUES_LAG = 5
-TRANSPOSE_LAG = 10
-QUANTISE_LAG = 11
-PV_LAG = 12
-STORE_LAG = 13
-LOAD_KEYS_AHEAD = 17
-LOAD_QUERIES_AHEAD = 10
-LOAD_VALUES_AHEAD = 8
-KEY_LOADS = 4
-FIRST_STEP = -KEYS_AHEAD
-LAST_STEP = ALL_TILES - 1 + STORE_LAG
+KEYS_DUE = 4
+VALUES_AHEAD = 7
+QUANTISE_LAG = 3
+SCALAR_SCALES = 24
+VECTOR_SQUARES = 4
+
+
+def squared_by_vector(b, j):
+    return b < B - 1 and j % VECTOR_SQUARES == VECTOR_SQUARES - 1
+
+
+def scalar_plan():
+    squares = [(FIRST_STEP, ("k", 0, j)) for j in range(TILES_PER_BANK)]
+    squares += [(FIRST_STEP + 1, ("q", 0))]
+    squares += [(FIRST_STEP + 2, ("k", 0, j)) for j in range(TILES_PER_BANK, TILES)]
+    rest = [(n - 2, ("q", n)) for n in range(1, ALL_TILES)]
+    rest += [(TILES * b - KEYS_DUE + j // 4, ("k", b, j)) for b in range(1, B) for j in range(TILES)]
+    squares += sorted(rest, key=lambda item: item[0])
+    passes = []
+    for first in range(0, ALL_TILES, GROUP):
+        passes += [("root", n) for n in range(first, first + GROUP)]
+        passes += [("exp", n) for n in range(first, first + GROUP)]
+
+    def load_of(item):
+        return 0 if item[0] == "k" and squared_by_vector(item[1], item[2]) else 1
+
+    plan = {}
+    step = FIRST_STEP
+    s = 0
+    a = 0
+    while s < len(squares) or a < len(passes):
+        plan[step] = []
+        load = 0
+        while s < len(squares) and squares[s][0] <= step:
+            plan[step] += [squares[s][1]]
+            load += load_of(squares[s][1])
+            s += 1
+        while a < len(passes) and load + 2 <= SCALAR_LOAD and (passes[a][0] == "exp" or passes[a][1] <= step - ROOT_LAG):
+            plan[step] += [passes[a]]
+            load += 2
+            a += 1
+        while s < len(squares) and load < SCALAR_LOAD and squares[s][0] <= step + SQUARES_AHEAD:
+            plan[step] += [squares[s][1]]
+            load += load_of(squares[s][1])
+            s += 1
+        step += 1
+    return plan
+
+
+def transpose_steps(plan):
+    steps = {}
+    for step, items in plan.items():
+        for item in items:
+            if item[0] == "exp":
+                steps[item[1]] = max(step + 1, steps.get(item[1] - 1, step) + 1)
+    return steps
+
+
+def transpose_plan(steps):
+    plan = {
+        (FIRST_STEP, 0): ("k", 0, 0),
+        (FIRST_STEP, 1): ("k", 0, 1),
+        (FIRST_STEP + 1, 0): ("q", 0),
+        (FIRST_STEP + 1, 1): ("k", 0, 2),
+        (FIRST_STEP + 2, 0): ("k", 0, 3),
+    }
+    for n in range(PAIR, ALL_TILES, PAIR):
+        plan[n - QUERY_AHEAD, 0] = ("q", n // PAIR)
+    for n, step in steps.items():
+        plan[step, 1] = ("e", n)
+    half = 1
+    for b in range(1, B):
+        for pair in range(TILES // PAIR):
+            while divmod(half, HALVES) in plan:
+                half += 1
+            plan[divmod(half, HALVES)] = ("k", b, pair)
+    return plan
 
 
 def tile_qkvattention_pa_t_kernel(tc, q_scaled, k_scaled, v, out):
@@ -55,18 +120,21 @@ def tile_qkvattention_pa_t_kernel(tc, q_scaled, k_scaled, v, out):
         psum = stack.enter_context(tc.psum_pool(name="psum", bufs=1))
         stack.enter_context(tc.manual_schedule())
 
+        plan = scalar_plan()
+        t_step = transpose_steps(plan)
+        t_tile = {step: n for n, step in t_step.items()}
+        jobs = transpose_plan(t_step)
+        last_step = t_step[ALL_TILES - 1] + 3
+
         identity = sbuf.tile([P, P], F32, name="identity")
         make_identity(nc, identity[:])
 
         q_rows, k_rows, v_rows = {}, {}, {}
         q2, z_cap, k2, bank_start, k_t = {}, {}, {}, {}, {}
-        z_max, d2_min, dist, dist_min, row_sum, row_scale = {}, {}, {}, {}, {}, {}
+        z_max, d2_min, dist_min, row_sum, row_scale = {}, {}, {}, {}, {}
         v_grouped, v_codes, v_scales = {}, {}, {}
-        q_t, z, e, e_bank, e_grouped, e_codes, e_scales, acc = {}, {}, {}, {}, {}, {}, {}, {}
+        q_t, z, e, e_grouped, e_codes, e_scales, acc = {}, {}, {}, {}, {}, {}, {}
         s_bank, t_bank = {}, {}
-
-        def is_batch(b):
-            return 0 <= b < B
 
         def is_tile(n):
             return 0 <= n < ALL_TILES
@@ -74,36 +142,60 @@ def tile_qkvattention_pa_t_kernel(tc, q_scaled, k_scaled, v, out):
         def is_bank(m):
             return 0 <= m < ALL_BANKS
 
-        def transpose_bank(name):
-            return psum.tile([P, PAIR, PAIR, P], F32, name=name, tag="transposes", bufs=3)
+        def load_keys(b, first, last):
+            if first == 0:
+                k_rows[b] = sbuf.tile([P, TILES, C], BF16, name="k_rows", tag="k_rows", bufs=B)
+            source = k_scaled[b].rearrange("(i p) c -> p i c", p=P)
+            nc.sync.dma_start(out=k_rows[b][:, first:last, :], in_=source[:, first:last, :])
+
+        def load_queries(b, first, last):
+            if first == 0:
+                q_rows[b] = sbuf.tile([P, TILES, C], BF16, name="q_rows", tag="q_rows", bufs=2)
+            source = q_scaled[b].rearrange("(i p) c -> p i c", p=P)
+            nc.sync.dma_start(out=q_rows[b][:, first:last, :], in_=source[:, first:last, :])
+
+        def load_values(b):
+            v_rows[b] = sbuf.tile([P, PASSES, PACK, C], BF16, name="v_rows", tag="v_rows", bufs=2)
+            nc.sync.dma_start(
+                out=v_rows[b][:].rearrange("p g (u w) c -> p (g u) (w c)", w=PAIR),
+                in_=v[b].rearrange("(a p w) c -> p a (w c)", p=P, w=PAIR),
+            )
 
         def load_inputs(step):
-            for b in range(B):
-                if step == max(FIRST_STEP, TILES * b - LOAD_KEYS_AHEAD):
-                    k_rows[b] = sbuf.tile([P, TILES, C], BF16, name="k_rows", tag="k_rows", bufs=2)
-                    source = k_scaled[b].rearrange("(i p) c -> p i c", p=P)
-                    for part in range(KEY_LOADS):
-                        tiles = slice(part * TILES // KEY_LOADS, (part + 1) * TILES // KEY_LOADS)
-                        nc.sync.dma_start(out=k_rows[b][:, tiles, :], in_=source[:, tiles, :])
-                if step == max(FIRST_STEP, TILES * b - LOAD_QUERIES_AHEAD):
-                    q_rows[b] = sbuf.tile([P, TILES, C], BF16, name="q_rows", tag="q_rows", bufs=2)
-                    nc.sync.dma_start(out=q_rows[b][:], in_=q_scaled[b].rearrange("(i p) c -> p i c", p=P))
-                if step == max(FIRST_STEP, TILES * b - LOAD_VALUES_AHEAD):
-                    v_rows[b] = sbuf.tile([P, PASSES, PACK, C], BF16, name="v_rows", tag="v_rows", bufs=2)
-                    nc.sync.dma_start(
-                        out=v_rows[b][:].rearrange("p g (u w) c -> p (g u) (w c)", w=PAIR),
-                        in_=v[b].rearrange("(a p w) c -> p a (w c)", p=P, w=PAIR),
-                    )
+            if step == FIRST_STEP:
+                load_keys(0, 0, 2)
+                load_keys(0, 2, 4)
+                load_queries(0, 0, 2)
+                load_keys(0, 4, 6)
+                load_keys(0, 6, 8)
+                load_queries(0, 2, 8)
+                load_keys(1, 0, 8)
+                load_values(0)
+                load_queries(1, 0, 8)
+                load_keys(2, 0, 8)
+                load_keys(3, 0, 8)
+                load_values(1)
+            for b in (2, 3):
+                if step == TILES * (b - 1) - 3:
+                    load_queries(b, 0, 8)
+                if step == t_step[TILES * (b - 2)] + 1:
+                    load_values(b)
 
-        def sum_of_squares(rows, total):
+        def sum_of_squares(rows, total, vec=False):
+            if vec:
+                squares = sbuf.tile([P, C], F32, name="squares2", tag="squares2", bufs=2)
+                nc.vector.scalar_tensor_tensor(
+                    out=squares[:], in0=rows, scalar=1.0, in1=rows, op0=ALU.mult, op1=ALU.mult, accum_out=total
+                )
+                return
             squares = sbuf.tile([P, C], BF16, name="squares", tag="squares", bufs=4)
             nc.scalar.activation(out=squares[:], in_=rows, func=ACT.Square, accum_out=total)
 
         def query_norm(n):
             b, i = divmod(n, TILES)
             if i == 0:
-                q2[b] = sbuf.tile([P, TILES], F32, name="q2", tag="q2", bufs=2)
-                z_cap[b] = sbuf.tile([P, TILES], F32, name="z_cap", tag="z_cap", bufs=2)
+                q2[b] = sbuf.tile([P, TILES], F32, name="q2", tag="q2", bufs=3)
+                z_cap[b] = sbuf.tile([P, TILES], F32, name="z_cap", tag="z_cap", bufs=3)
             sum_of_squares(q_rows[b][:, i, :], q2[b][:, i : i + 1])
             nc.gpsimd.tensor_scalar(
                 out=z_cap[b][:, i : i + 1],
@@ -117,8 +209,8 @@ def tile_qkvattention_pa_t_kernel(tc, q_scaled, k_scaled, v, out):
         def key_norm(b, j):
             if j == 0:
                 k2[b] = sbuf.tile([P, TILES], F32, name="k2", tag="k2", bufs=2)
-                bank_start[b] = sbuf.tile([P, TILES], F32, name="bank_start", tag="bank_start", bufs=3)
-            sum_of_squares(k_rows[b][:, j, :], k2[b][:, j : j + 1])
+                bank_start[b] = sbuf.tile([P, TILES], F32, name="bank_start", tag="bank_start", bufs=4)
+            sum_of_squares(k_rows[b][:, j, :], k2[b][:, j : j + 1], squared_by_vector(b, j))
             nc.gpsimd.tensor_scalar(
                 out=bank_start[b][:, j : j + 1],
                 in0=k2[b][:, j : j + 1],
@@ -128,33 +220,47 @@ def tile_qkvattention_pa_t_kernel(tc, q_scaled, k_scaled, v, out):
                 op1=ALU.add,
             )
 
-        def transpose_operand(step, number):
-            n = step + QUERY_AHEAD
-            b_k, j = divmod(step + KEYS_AHEAD, TILES)
-            if number == 0 and (is_tile(n) or is_batch(b_k)):
-                t_bank[step] = transpose_bank("t_bank")
-            side, u = divmod(number, PAIR)
+        def transpose_part(step, h, r):
+            job = jobs.get((step, h))
+            if job is None:
+                return
+            if r == 0:
+                t_bank[step, h] = psum.tile([P, PAIR, PAIR, P], F32, name="t_bank", tag="transposes", bufs=3)
+            a, u = divmod(r, PAIR)
             words = slice(u * P, (u + 1) * P)
-            if side == 0 and is_tile(n):
-                b, i = divmod(n, TILES)
-                nc.tensor.transpose(
-                    out=t_bank[step][:, 0, u, :], in_=q_rows[b][:, i, :].bitcast(F32)[:, words], identity=identity[:]
-                )
-            if side == 1 and is_batch(b_k):
-                nc.tensor.transpose(
-                    out=t_bank[step][:, 1, u, :], in_=k_rows[b_k][:, j, :].bitcast(F32)[:, words], identity=identity[:]
-                )
+            if job[0] == "q":
+                b, i = divmod(PAIR * job[1] + a, TILES)
+                source = q_rows[b][:, i, :].bitcast(F32)[:, words]
+            elif job[0] == "k":
+                source = k_rows[job[1]][:, PAIR * job[2] + a, :].bitcast(F32)[:, words]
+            else:
+                source = e[job[1]][:].bitcast(F32)[:, r * P : (r + 1) * P]
+            nc.tensor.transpose(out=t_bank[step, h][:, a, u, :], in_=source, identity=identity[:])
 
-        def copy_operands(step):
-            n = step + QUERY_AHEAD
-            b_k, j = divmod(step + KEYS_AHEAD, TILES)
-            if is_tile(n):
-                q_t[n] = sbuf.tile([P, PAIR, P], F32, name="q_t", tag="q_t", bufs=4)
-                nc.vector.tensor_copy(out=q_t[n][:], in_=t_bank[step][:, 0])
-            if is_batch(b_k):
+        def copy_job(step, h):
+            job = jobs.get((step, h))
+            if job is None:
+                return
+            bank = t_bank[step, h]
+            if job[0] == "q":
+                pair = sbuf.tile([P, PAIR, PAIR, P], F32, name="q_t", tag="q_t", bufs=3)
+                nc.vector.tensor_copy(out=pair[:], in_=bank[:])
+                for a in range(PAIR):
+                    q_t[PAIR * job[1] + a] = pair[:, a]
+            elif job[0] == "k":
+                b, j = job[1], job[2]
                 if j == 0:
-                    k_t[b_k] = sbuf.tile([P, PAIR, T], F32, name="k_t", tag="k_t", bufs=2)
-                nc.vector.tensor_copy(out=k_t[b_k][:, :, j * P : (j + 1) * P], in_=t_bank[step][:, 1])
+                    k_t[b] = sbuf.tile([P, PAIR, T], F32, name="k_t", tag="k_t", bufs=B)
+                cols = slice(j * PAIR * P, (j + 1) * PAIR * P)
+                nc.vector.tensor_copy(
+                    out=k_t[b][:, :, cols].rearrange("p u (a s) -> p u a s", a=PAIR), in_=bank[:].rearrange("p a u s -> p u a s")
+                )
+            else:
+                n = job[1]
+                e_grouped[n] = sbuf.tile(
+                    [P, PASSES, P, PACK], BF16, name="e_grouped", tag="e_grouped", bufs=3, align_bytes=64
+                )
+                nc.vector.tensor_copy(out=e_grouped[n][:].bitcast(F32), in_=bank[:].rearrange("p g u t -> p g t u"))
 
         def start_bank(m, r):
             n, h = divmod(m, HALVES)
@@ -173,7 +279,7 @@ def tile_qkvattention_pa_t_kernel(tc, q_scaled, k_scaled, v, out):
         def score_matmul(m, c):
             n, h = divmod(m, HALVES)
             u, w = divmod(c, PAIR)
-            queries = q_t[n][:].bitcast(BF16).rearrange("p u (t w) -> p u t w", w=PAIR)
+            queries = q_t[n].bitcast(BF16).rearrange("p u (t w) -> p u t w", w=PAIR)
             keys = k_t[n // TILES][:].bitcast(BF16).rearrange("p u (s w) -> p u s w", w=PAIR)
             nc.tensor.matmul(
                 out=s_bank[m][:],
@@ -187,9 +293,9 @@ def tile_qkvattention_pa_t_kernel(tc, q_scaled, k_scaled, v, out):
             n, h = divmod(m, HALVES)
             b, i = divmod(n, TILES)
             if i == 0 and h == 0:
-                z_max[b] = sbuf.tile([P, TILES, HALVES], F32, name="z_max", tag="z_max", bufs=2)
+                z_max[b] = sbuf.tile([P, TILES, HALVES], F32, name="z_max", tag="z_max", bufs=3)
             if h == 0:
-                z[n] = sbuf.tile([P, T], F32, name="z", tag="z", bufs=7)
+                z[n] = sbuf.tile([P, T], F32, name="z", tag="z", bufs=16)
             nc.vector.tensor_scalar(
                 out=z[n][:, h * BANK : (h + 1) * BANK],
                 in0=s_bank[m][:],
@@ -200,44 +306,40 @@ def tile_qkvattention_pa_t_kernel(tc, q_scaled, k_scaled, v, out):
                 accum_out=z_max[b][:, i, h : h + 1],
             )
 
-        def nearest_keys(b):
+        def nearest_keys(n):
+            b = n // TILES
             d2_min[b] = sbuf.tile([P, TILES], F32, name="d2_min", tag="d2_min", bufs=2)
             nc.vector.tensor_reduce(out=d2_min[b][:], in_=z_max[b][:], axis=mybir.AxisListType.X, op=ALU.max)
             nc.vector.scalar_tensor_tensor(
                 out=d2_min[b][:], in0=d2_min[b][:], scalar=-2.0, in1=q2[b][:], op0=ALU.mult, op1=ALU.add
             )
 
-        def roots(b, first_tile):
-            if first_tile == 0:
-                dist[b] = sbuf.tile([P, TILES, T], F32, name="dist", tag="dist", bufs=1)
-            for i in range(first_tile, first_tile + TILES_PER_PHASE_STEP):
-                nc.scalar.activation(
-                    out=dist[b][:, i, :], in_=z[TILES * b + i][:], func=ACT.Sqrt, scale=-2.0, bias=q2[b][:, i : i + 1]
-                )
-            if first_tile + TILES_PER_PHASE_STEP == TILES:
+        def root(n):
+            b, i = divmod(n, TILES)
+            nc.scalar.activation(out=z[n][:], in_=z[n][:], func=ACT.Sqrt, scale=-2.0, bias=q2[b][:, i : i + 1])
+            if i == TILES - 1:
                 dist_min[b] = sbuf.tile([P, TILES], F32, name="dist_min", tag="dist_min", bufs=2)
                 nc.scalar.activation(out=dist_min[b][:], in_=d2_min[b][:], func=ACT.Sqrt)
 
-        def exps(b, first_tile):
-            if first_tile == 0:
+        def exp(n):
+            b, i = divmod(n, TILES)
+            if i == 0:
                 row_sum[b] = sbuf.tile([P, TILES], F32, name="row_sum", tag="row_sum", bufs=2)
-            for i in range(first_tile, first_tile + TILES_PER_PHASE_STEP):
-                n = TILES * b + i
-                e[n] = sbuf.tile([P, T], BF16, name="e", tag="e", bufs=7)
-                nc.scalar.activation(
-                    out=e[n][:],
-                    in_=dist[b][:, i, :],
-                    func=ACT.Exp,
-                    scale=-1.0,
-                    bias=dist_min[b][:, i : i + 1],
-                    accum_out=row_sum[b][:, i : i + 1],
-                )
+            e[n] = sbuf.tile([P, T], BF16, name="e", tag="e", bufs=8)
+            nc.scalar.activation(
+                out=e[n][:],
+                in_=z[n][:],
+                func=ACT.Exp,
+                scale=-1.0,
+                bias=dist_min[b][:, i : i + 1],
+                accum_out=row_sum[b][:, i : i + 1],
+            )
 
-        def reciprocals(b, first_tile):
-            if first_tile == 0:
+        def row_reciprocal(n):
+            b, i = divmod(n, TILES)
+            if i == 0:
                 row_scale[b] = sbuf.tile([P, TILES], F32, name="row_scale", tag="row_scale", bufs=2)
-            tiles = slice(first_tile, first_tile + TILES_PER_PHASE_STEP)
-            nc.vector.reciprocal(out=row_scale[b][:, tiles], in_=row_sum[b][:, tiles])
+            nc.vector.reciprocal(out=row_scale[b][:, i : i + 1], in_=row_sum[b][:, i : i + 1])
 
         def regroup_values(b, g):
             if g == 0:
@@ -259,18 +361,6 @@ def tile_qkvattention_pa_t_kernel(tc, q_scaled, k_scaled, v, out):
                 scales=v_scales[b][:, g, :],
                 in_=v_grouped[b, g][:].rearrange("p c j -> p (c j)"),
             )
-
-        def transpose_e(n, a):
-            if a == 0:
-                e_bank[n] = transpose_bank("e_bank")
-            g, u = divmod(a, PAIR)
-            nc.tensor.transpose(
-                out=e_bank[n][:, g, u, :], in_=e[n][:].bitcast(F32)[:, a * P : (a + 1) * P], identity=identity[:]
-            )
-
-        def copy_e(n):
-            e_grouped[n] = sbuf.tile([P, PASSES, P, PACK], BF16, name="e_grouped", tag="e_grouped", bufs=3, align_bytes=64)
-            nc.vector.tensor_copy(out=e_grouped[n][:].bitcast(F32), in_=e_bank[n][:].rearrange("p g u t -> p g t u"))
 
         def quantise_e(n):
             e_codes[n] = sbuf.tile([P, PASSES, P], U32, name="e_codes", tag="e_codes", bufs=3, align_bytes=64)
@@ -298,22 +388,22 @@ def tile_qkvattention_pa_t_kernel(tc, q_scaled, k_scaled, v, out):
         def scale_and_store(n):
             b, i = divmod(n, TILES)
             out_rows = sbuf.tile([P, C], F32, name="out_rows", tag="out_rows", bufs=4)
-            nc.vector.tensor_scalar(
-                out=out_rows[:], in0=acc[n][:], scalar1=row_scale[b][:, i : i + 1], scalar2=None, op0=ALU.mult
-            )
+            if n >= SCALAR_SCALES:
+                nc.scalar.activation(out=out_rows[:], in_=acc[n][:], func=ACT.Copy, scale=row_scale[b][:, i : i + 1])
+            else:
+                nc.vector.tensor_scalar(
+                    out=out_rows[:], in0=acc[n][:], scalar1=row_scale[b][:, i : i + 1], scalar2=None, op0=ALU.mult
+                )
             nc.sync.dma_start(out=out[b, i * P : (i + 1) * P, :], in_=out_rows[:])
 
-        for step in range(FIRST_STEP, LAST_STEP + 1):
+        for step in range(FIRST_STEP, last_step + 1):
             load_inputs(step)
-            phase_batch, phase_step = divmod(step - PHASE_LAG, TILES)
-            if is_batch(phase_batch) and phase_step == PHASE_STEPS - 1:
-                nearest_keys(phase_batch)
-            b, j = divmod(step + KEYS_AHEAD, TILES)
-            if is_batch(b):
-                key_norm(b, j)
-            if is_tile(step + QUERY_AHEAD):
-                query_norm(step + QUERY_AHEAD)
-
+            for todo in plan.get(step, []):
+                if todo[0] == "k":
+                    key_norm(todo[1], todo[2])
+                elif todo[0] == "q":
+                    query_norm(todo[1])
+            done = t_tile.get(step - 1)
             for h in range(HALVES):
                 m = HALVES * step + h
                 for c in range(CHUNKS):
@@ -321,36 +411,29 @@ def tile_qkvattention_pa_t_kernel(tc, q_scaled, k_scaled, v, out):
                         score_matmul(m, c)
                     if is_bank(m + 1):
                         start_bank(m + 1, c)
-                    if h == 0:
-                        transpose_operand(step, c)
-                    elif is_tile(step - TRANSPOSE_LAG):
-                        transpose_e(step - TRANSPOSE_LAG, c)
+                    transpose_part(step, h, c)
                 if is_bank(m):
                     cap_and_maximum(m)
-                if h == 0:
-                    copy_operands(step)
-                elif is_tile(step - TRANSPOSE_LAG):
-                    copy_e(step - TRANSPOSE_LAG)
-
-            if is_batch(phase_batch):
-                if phase_step < PHASE_STEPS:
-                    roots(phase_batch, phase_step * TILES_PER_PHASE_STEP)
-                else:
-                    exps(phase_batch, (phase_step - PHASE_STEPS) * TILES_PER_PHASE_STEP)
-            b, pair = divmod(step - PHASE_LAG - PHASE_STEPS - RECIPROCAL_LAG, TILES)
-            if is_batch(b) and pair < PHASE_STEPS:
-                reciprocals(b, pair * TILES_PER_PHASE_STEP)
-
-            if is_tile(step - QUANTISE_LAG):
-                quantise_e(step - QUANTISE_LAG)
-            if is_tile(step - PV_LAG):
-                multiply_with_values(step - PV_LAG)
-            if is_tile(step - STORE_LAG):
-                scale_and_store(step - STORE_LAG)
-
-            b, part = divmod(step - VALUES_LAG, TILES)
-            if is_batch(b) and part < 2 * PASSES:
-                if part % 2 == 0:
-                    regroup_values(b, part // 2)
-                else:
-                    quantise_values(b, part // 2)
+                    if h == 1 and step % TILES == TILES - 1:
+                        nearest_keys(step)
+                copy_job(step, h)
+            if t_tile.get(step - 3, -1) >= SCALAR_SCALES:
+                scale_and_store(t_tile[step - 3])
+            for todo in plan.get(step, []):
+                if todo[0] == "root":
+                    root(todo[1])
+                elif todo[0] == "exp":
+                    exp(todo[1])
+            if done is not None:
+                quantise_e(done)
+                row_reciprocal(done)
+            if t_tile.get(step - 2) is not None:
+                multiply_with_values(t_tile[step - 2])
+            if t_tile.get(step - 3) is not None and t_tile[step - 3] < SCALAR_SCALES:
+                scale_and_store(t_tile[step - 3])
+            for b in range(B):
+                for g in range(PASSES):
+                    if step == t_step[TILES * b] - VALUES_AHEAD + 2 * g:
+                        regroup_values(b, g)
+                    if step == t_step[TILES * b] - VALUES_AHEAD + QUANTISE_LAG + 2 * g:
+                        quantise_values(b, g)

@@ -37,7 +37,7 @@ QUERY_AHEAD = 2
 KEYS_DUE = 4
 VALUES_AHEAD = 7
 QUANTISE_LAG = 3
-SCALAR_SCALES = 24
+SCALAR_SCALES = 26
 VECTOR_SQUARES = 4
 
 
@@ -207,8 +207,8 @@ def tile_qkvattention_pa_t_kernel(tc, q_scaled, k_scaled, v, out):
             )
 
         def key_norm(b, j):
-            if j == 0:
-                k2[b] = sbuf.tile([P, TILES], F32, name="k2", tag="k2", bufs=2)
+            if b not in k2:
+                k2[b] = sbuf.tile([P, TILES], F32, name="k2", tag="k2", bufs=3)
                 bank_start[b] = sbuf.tile([P, TILES], F32, name="bank_start", tag="bank_start", bufs=4)
             sum_of_squares(k_rows[b][:, j, :], k2[b][:, j : j + 1], squared_by_vector(b, j))
             nc.gpsimd.tensor_scalar(
@@ -251,6 +251,9 @@ def tile_qkvattention_pa_t_kernel(tc, q_scaled, k_scaled, v, out):
                 b, j = job[1], job[2]
                 if j == 0:
                     k_t[b] = sbuf.tile([P, PAIR, T], F32, name="k_t", tag="k_t", bufs=B)
+                for i in range(PAIR * j, PAIR * (j + 1)):
+                    if b > 0 and squared_by_vector(b, i):
+                        key_norm(b, i)
                 cols = slice(j * PAIR * P, (j + 1) * PAIR * P)
                 nc.vector.tensor_copy(
                     out=k_t[b][:, :, cols].rearrange("p u (a s) -> p u a s", a=PAIR), in_=bank[:].rearrange("p a u s -> p u a s")
@@ -339,7 +342,8 @@ def tile_qkvattention_pa_t_kernel(tc, q_scaled, k_scaled, v, out):
             b, i = divmod(n, TILES)
             if i == 0:
                 row_scale[b] = sbuf.tile([P, TILES], F32, name="row_scale", tag="row_scale", bufs=2)
-            nc.vector.reciprocal(out=row_scale[b][:, i : i + 1], in_=row_sum[b][:, i : i + 1])
+            if i % PAIR == PAIR - 1:
+                nc.vector.reciprocal(out=row_scale[b][:, i - 1 : i + 1], in_=row_sum[b][:, i - 1 : i + 1])
 
         def regroup_values(b, g):
             if g == 0:
@@ -399,24 +403,31 @@ def tile_qkvattention_pa_t_kernel(tc, q_scaled, k_scaled, v, out):
         for step in range(FIRST_STEP, last_step + 1):
             load_inputs(step)
             for todo in plan.get(step, []):
-                if todo[0] == "k":
+                if todo[0] == "k" and not (todo[1] > 0 and squared_by_vector(todo[1], todo[2])):
                     key_norm(todo[1], todo[2])
                 elif todo[0] == "q":
                     query_norm(todo[1])
             done = t_tile.get(step - 1)
             for h in range(HALVES):
                 m = HALVES * step + h
+                product = t_tile.get(step - 3) if h == 0 and is_bank(m) else None
                 for c in range(CHUNKS):
                     if is_bank(m):
                         score_matmul(m, c)
-                    if is_bank(m + 1):
-                        start_bank(m + 1, c)
-                    transpose_part(step, h, c)
+                    if product is not None and c == 0:
+                        multiply_with_values(product)
+                        continue
+                    for r in (0, 1) if product is not None and c == 1 else (c,):
+                        if is_bank(m + 1):
+                            start_bank(m + 1, r)
+                        transpose_part(step, h, r)
                 if is_bank(m):
                     cap_and_maximum(m)
                     if h == 1 and step % TILES == TILES - 1:
                         nearest_keys(step)
                 copy_job(step, h)
+                if h == 0 and step < ALL_TILES and -1 < t_tile.get(step - 3, -1) < SCALAR_SCALES:
+                    scale_and_store(t_tile[step - 3])
             if t_tile.get(step - 3, -1) >= SCALAR_SCALES:
                 scale_and_store(t_tile[step - 3])
             for todo in plan.get(step, []):
@@ -427,9 +438,11 @@ def tile_qkvattention_pa_t_kernel(tc, q_scaled, k_scaled, v, out):
             if done is not None:
                 quantise_e(done)
                 row_reciprocal(done)
-            if t_tile.get(step - 2) is not None:
+            if step == ALL_TILES and t_tile.get(step - 3) is not None:
+                multiply_with_values(t_tile[step - 3])
+            if step >= ALL_TILES and t_tile.get(step - 2) is not None:
                 multiply_with_values(t_tile[step - 2])
-            if t_tile.get(step - 3) is not None and t_tile[step - 3] < SCALAR_SCALES:
+            if step >= ALL_TILES and -1 < t_tile.get(step - 3, -1) < SCALAR_SCALES:
                 scale_and_store(t_tile[step - 3])
             for b in range(B):
                 for g in range(PASSES):

@@ -408,19 +408,17 @@ def tile_qkvattention_pa_t_kernel(tc, q_scaled, k_scaled, v, out):
                 elif todo[0] == "q":
                     query_norm(todo[1])
             done = t_tile.get(step - 1)
+            if done is not None:
+                quantise_e(done)
+                row_reciprocal(done)
             for h in range(HALVES):
                 m = HALVES * step + h
-                product = t_tile.get(step - 3) if h == 0 and is_bank(m) else None
                 for c in range(CHUNKS):
                     if is_bank(m):
                         score_matmul(m, c)
-                    if product is not None and c == 0:
-                        multiply_with_values(product)
-                        continue
-                    for r in (0, 1) if product is not None and c == 1 else (c,):
-                        if is_bank(m + 1):
-                            start_bank(m + 1, r)
-                        transpose_part(step, h, r)
+                    if is_bank(m + 1):
+                        start_bank(m + 1, c)
+                    transpose_part(step, h, c)
                 if is_bank(m):
                     cap_and_maximum(m)
                     if h == 1 and step % TILES == TILES - 1:
@@ -435,12 +433,7 @@ def tile_qkvattention_pa_t_kernel(tc, q_scaled, k_scaled, v, out):
                     root(todo[1])
                 elif todo[0] == "exp":
                     exp(todo[1])
-            if done is not None:
-                quantise_e(done)
-                row_reciprocal(done)
-            if step == ALL_TILES and t_tile.get(step - 3) is not None:
-                multiply_with_values(t_tile[step - 3])
-            if step >= ALL_TILES and t_tile.get(step - 2) is not None:
+            if t_tile.get(step - 2) is not None:
                 multiply_with_values(t_tile[step - 2])
             if step >= ALL_TILES and -1 < t_tile.get(step - 3, -1) < SCALAR_SCALES:
                 scale_and_store(t_tile[step - 3])

@@ -309,10 +309,11 @@ def tile_qkvattention_pa_t_kernel(tc, q_scaled, k_scaled, v, out):
                 accum_out=z_max[b][:, i, h : h + 1],
             )
 
-        def nearest_keys(n):
-            b = n // TILES
+        def nearest_keys(b):
             d2_min[b] = sbuf.tile([P, TILES], F32, name="d2_min", tag="d2_min", bufs=2)
             nc.vector.tensor_reduce(out=d2_min[b][:], in_=z_max[b][:], axis=mybir.AxisListType.X, op=ALU.max)
+
+        def nearest_distances(b):
             nc.vector.scalar_tensor_tensor(
                 out=d2_min[b][:], in0=d2_min[b][:], scalar=-2.0, in1=q2[b][:], op0=ALU.mult, op1=ALU.add
             )
@@ -408,9 +409,6 @@ def tile_qkvattention_pa_t_kernel(tc, q_scaled, k_scaled, v, out):
                 elif todo[0] == "q":
                     query_norm(todo[1])
             done = t_tile.get(step - 1)
-            if done is not None:
-                quantise_e(done)
-                row_reciprocal(done)
             for h in range(HALVES):
                 m = HALVES * step + h
                 for c in range(CHUNKS):
@@ -421,9 +419,9 @@ def tile_qkvattention_pa_t_kernel(tc, q_scaled, k_scaled, v, out):
                     transpose_part(step, h, c)
                 if is_bank(m):
                     cap_and_maximum(m)
-                    if h == 1 and step % TILES == TILES - 1:
-                        nearest_keys(step)
                 copy_job(step, h)
+                if h == 1 and is_tile(step) and step % TILES == TILES - 1:
+                    nearest_keys(step // TILES)
                 if h == 0 and step < ALL_TILES and -1 < t_tile.get(step - 3, -1) < SCALAR_SCALES:
                     scale_and_store(t_tile[step - 3])
             if t_tile.get(step - 3, -1) >= SCALAR_SCALES:
@@ -433,6 +431,12 @@ def tile_qkvattention_pa_t_kernel(tc, q_scaled, k_scaled, v, out):
                     root(todo[1])
                 elif todo[0] == "exp":
                     exp(todo[1])
+            if done is not None:
+                quantise_e(done)
+            if is_tile(step) and step % TILES == TILES - 1:
+                nearest_distances(step // TILES)
+            if done is not None:
+                row_reciprocal(done)
             if t_tile.get(step - 2) is not None:
                 multiply_with_values(t_tile[step - 2])
             if step >= ALL_TILES and -1 < t_tile.get(step - 3, -1) < SCALAR_SCALES:

@@ -126,7 +126,7 @@ def tile_qkvattention_pa_t_kernel(tc, q_scaled, k_scaled, v, out):
         jobs = transpose_plan(t_step)
         last_step = t_step[ALL_TILES - 1] + 3
 
-        identity = sbuf.tile([P, P], F32, name="identity")
+        identity = sbuf.tile([P, P], F32, name="identity", align_bytes=256)
         make_identity(nc, identity[:])
 
         q_rows, k_rows, v_rows = {}, {}, {}
@@ -144,13 +144,13 @@ def tile_qkvattention_pa_t_kernel(tc, q_scaled, k_scaled, v, out):
 
         def load_keys(b, first, last):
             if first == 0:
-                k_rows[b] = sbuf.tile([P, TILES, C], BF16, name="k_rows", tag="k_rows", bufs=B)
+                k_rows[b] = sbuf.tile([P, TILES, C], BF16, name="k_rows", tag="k_rows", bufs=B, align_bytes=256)
             source = k_scaled[b].rearrange("(i p) c -> p i c", p=P)
             nc.sync.dma_start(out=k_rows[b][:, first:last, :], in_=source[:, first:last, :])
 
         def load_queries(b, first, last):
             if first == 0:
-                q_rows[b] = sbuf.tile([P, TILES, C], BF16, name="q_rows", tag="q_rows", bufs=2)
+                q_rows[b] = sbuf.tile([P, TILES, C], BF16, name="q_rows", tag="q_rows", bufs=2, align_bytes=256)
             source = q_scaled[b].rearrange("(i p) c -> p i c", p=P)
             nc.sync.dma_start(out=q_rows[b][:, first:last, :], in_=source[:, first:last, :])
 
@@ -243,14 +243,14 @@ def tile_qkvattention_pa_t_kernel(tc, q_scaled, k_scaled, v, out):
                 return
             bank = t_bank[step, h]
             if job[0] == "q":
-                pair = sbuf.tile([P, PAIR, PAIR, P], F32, name="q_t", tag="q_t", bufs=3)
+                pair = sbuf.tile([P, PAIR, PAIR, P], F32, name="q_t", tag="q_t", bufs=3, align_bytes=256)
                 nc.vector.tensor_copy(out=pair[:], in_=bank[:])
                 for a in range(PAIR):
                     q_t[PAIR * job[1] + a] = pair[:, a]
             elif job[0] == "k":
                 b, j = job[1], job[2]
                 if j == 0:
-                    k_t[b] = sbuf.tile([P, PAIR, T], F32, name="k_t", tag="k_t", bufs=B)
+                    k_t[b] = sbuf.tile([P, PAIR, T], F32, name="k_t", tag="k_t", bufs=B, align_bytes=256)
                 for i in range(PAIR * j, PAIR * (j + 1)):
                     if b > 0 and squared_by_vector(b, i):
                         key_norm(b, i)
@@ -261,7 +261,7 @@ def tile_qkvattention_pa_t_kernel(tc, q_scaled, k_scaled, v, out):
             else:
                 n = job[1]
                 e_grouped[n] = sbuf.tile(
-                    [P, PASSES, P, PACK], BF16, name="e_grouped", tag="e_grouped", bufs=3, align_bytes=64
+                    [P, PASSES, P, PACK], BF16, name="e_grouped", tag="e_grouped", bufs=3, align_bytes=256
                 )
                 nc.vector.tensor_copy(out=e_grouped[n][:].bitcast(F32), in_=bank[:].rearrange("p g u t -> p g t u"))
 
@@ -298,7 +298,7 @@ def tile_qkvattention_pa_t_kernel(tc, q_scaled, k_scaled, v, out):
             if i == 0 and h == 0:
                 z_max[b] = sbuf.tile([P, TILES, HALVES], F32, name="z_max", tag="z_max", bufs=3)
             if h == 0:
-                z[n] = sbuf.tile([P, T], F32, name="z", tag="z", bufs=16)
+                z[n] = sbuf.tile([P, T], F32, name="z", tag="z", bufs=16, align_bytes=256)
             nc.vector.tensor_scalar(
                 out=z[n][:, h * BANK : (h + 1) * BANK],
                 in0=s_bank[m][:],
@@ -329,7 +329,7 @@ def tile_qkvattention_pa_t_kernel(tc, q_scaled, k_scaled, v, out):
             b, i = divmod(n, TILES)
             if i == 0:
                 row_sum[b] = sbuf.tile([P, TILES], F32, name="row_sum", tag="row_sum", bufs=2)
-            e[n] = sbuf.tile([P, T], BF16, name="e", tag="e", bufs=8)
+            e[n] = sbuf.tile([P, T], BF16, name="e", tag="e", bufs=8, align_bytes=256)
             nc.scalar.activation(
                 out=e[n][:],
                 in_=z[n][:],
@@ -348,9 +348,9 @@ def tile_qkvattention_pa_t_kernel(tc, q_scaled, k_scaled, v, out):
 
         def regroup_values(b, g):
             if g == 0:
-                v_codes[b] = sbuf.tile([P, PASSES, C], U32, name="v_codes", tag="v_codes", bufs=2, align_bytes=64)
-                v_scales[b] = sbuf.tile([P, PASSES, C], U8, name="v_scales", tag="v_scales", bufs=2, align_bytes=64)
-            v_grouped[b, g] = sbuf.tile([P, C, PACK], BF16, name="v_grouped", tag="v_grouped", bufs=2, align_bytes=64)
+                v_codes[b] = sbuf.tile([P, PASSES, C], U32, name="v_codes", tag="v_codes", bufs=2, align_bytes=256)
+                v_scales[b] = sbuf.tile([P, PASSES, C], U8, name="v_scales", tag="v_scales", bufs=2, align_bytes=256)
+            v_grouped[b, g] = sbuf.tile([P, C, PACK], BF16, name="v_grouped", tag="v_grouped", bufs=2, align_bytes=256)
             nc.gpsimd.tensor_scalar(
                 out=v_grouped[b, g][:].rearrange("p (c r) j -> p c j r", r=4),
                 in0=v_rows[b][:, g].rearrange("p j (c r) -> p c j r", r=4),
@@ -368,8 +368,8 @@ def tile_qkvattention_pa_t_kernel(tc, q_scaled, k_scaled, v, out):
             )
 
         def quantise_e(n):
-            e_codes[n] = sbuf.tile([P, PASSES, P], U32, name="e_codes", tag="e_codes", bufs=3, align_bytes=64)
-            e_scales[n] = sbuf.tile([P, PASSES, P], U8, name="e_scales", tag="e_scales", bufs=3, align_bytes=64)
+            e_codes[n] = sbuf.tile([P, PASSES, P], U32, name="e_codes", tag="e_codes", bufs=3, align_bytes=256)
+            e_scales[n] = sbuf.tile([P, PASSES, P], U8, name="e_scales", tag="e_scales", bufs=3, align_bytes=256)
             nc.vector.quantize_mx(
                 out=e_codes[n][:].rearrange("p g t -> p (g t)").bitcast(FP8X4),
                 scales=e_scales[n][:].rearrange("p g t -> p (g t)"),

@@ -38,7 +38,8 @@ KEYS_DUE = 4
 VALUES_AHEAD = 7
 QUANTISE_LAG = 3
 SCALAR_SCALES = 26
-VECTOR_SQUARES = 4
+LAST_TILES = 28
+VECTOR_SQUARES = 2
 
 
 def squared_by_vector(b, j):
@@ -343,7 +344,9 @@ def tile_qkvattention_pa_t_kernel(tc, q_scaled, k_scaled, v, out):
             b, i = divmod(n, TILES)
             if i == 0:
                 row_scale[b] = sbuf.tile([P, TILES], F32, name="row_scale", tag="row_scale", bufs=2)
-            if i % PAIR == PAIR - 1:
+            if n >= LAST_TILES:
+                nc.vector.reciprocal(out=row_scale[b][:, i : i + 1], in_=row_sum[b][:, i : i + 1])
+            elif i % PAIR == PAIR - 1:
                 nc.vector.reciprocal(out=row_scale[b][:, i - 1 : i + 1], in_=row_sum[b][:, i - 1 : i + 1])
 
         def regroup_values(b, g):
@@ -378,7 +381,10 @@ def tile_qkvattention_pa_t_kernel(tc, q_scaled, k_scaled, v, out):
 
         def multiply_with_values(n):
             b = n // TILES
-            acc[n] = psum.tile([P, C], F32, name="acc", tag="acc", bufs=2)
+            if n < LAST_TILES:
+                acc[n] = psum.tile([P, C], F32, name="acc", tag="acc", bufs=2)
+            else:
+                acc[n] = psum.tile([P, C], F32, name="acc", tag="s_bank", bufs=3)
             for g in range(PASSES):
                 nc.tensor.matmul_mx(
                     out=acc[n][:],

@@ -29,16 +29,17 @@ D2_FLOOR = 2.0**-116
 D2_FLOOR_OF_Q2 = 2.0**-23
 
 FIRST_STEP = -3
-GROUP = 8
+GROUPS = (range(0, 11), range(11, 22), range(22, 32))
+GROUP_OF_LAST = {group[-1]: group for group in GROUPS}
 ROOT_LAG = 2
 SCALAR_LOAD = 5
 SQUARES_AHEAD = 8
 QUERY_AHEAD = 2
-KEYS_DUE = 4
+KEYS_DUE = 6
 VALUES_AHEAD = 7
 QUANTISE_LAG = 3
-SCALAR_SCALES = 26
-LAST_TILES = 28
+SCALAR_SCALES = 24
+LAST_TILES = 26
 VECTOR_SQUARES = 2
 
 
@@ -54,9 +55,9 @@ def scalar_plan():
     rest += [(TILES * b - KEYS_DUE + j // 4, ("k", b, j)) for b in range(1, B) for j in range(TILES)]
     squares += sorted(rest, key=lambda item: item[0])
     passes = []
-    for first in range(0, ALL_TILES, GROUP):
-        passes += [("root", n) for n in range(first, first + GROUP)]
-        passes += [("exp", n) for n in range(first, first + GROUP)]
+    for group in GROUPS:
+        passes += [("root", n) for n in group]
+        passes += [("exp", n) for n in group]
 
     def load_of(item):
         return 0 if item[0] == "k" and squared_by_vector(item[1], item[2]) else 1
@@ -131,8 +132,14 @@ def tile_qkvattention_pa_t_kernel(tc, q_scaled, k_scaled, v, out):
         make_identity(nc, identity[:])
 
         q_rows, k_rows, v_rows = {}, {}, {}
-        q2, z_cap, k2, bank_start, k_t = {}, {}, {}, {}, {}
-        z_max, d2_min, dist_min, row_sum, row_scale = {}, {}, {}, {}, {}
+        k2, bank_start, k_t = {}, {}, {}
+        q2 = sbuf.tile([P, ALL_TILES], F32, name="q2")
+        z_cap = sbuf.tile([P, ALL_TILES], F32, name="z_cap")
+        z_max = sbuf.tile([P, ALL_TILES, HALVES], F32, name="z_max")
+        d2_min = sbuf.tile([P, ALL_TILES], F32, name="d2_min")
+        dist_min = sbuf.tile([P, ALL_TILES], F32, name="dist_min")
+        row_sum = sbuf.tile([P, ALL_TILES], F32, name="row_sum")
+        row_scale = sbuf.tile([P, ALL_TILES], F32, name="row_scale")
         v_grouped, v_codes, v_scales = {}, {}, {}
         q_t, z, e, e_grouped, e_codes, e_scales, acc = {}, {}, {}, {}, {}, {}, {}
         s_bank, t_bank = {}, {}
@@ -189,18 +196,15 @@ def tile_qkvattention_pa_t_kernel(tc, q_scaled, k_scaled, v, out):
                     out=squares[:], in0=rows, scalar=1.0, in1=rows, op0=ALU.mult, op1=ALU.mult, accum_out=total
                 )
                 return
-            squares = sbuf.tile([P, C], BF16, name="squares", tag="squares", bufs=4)
+            squares = sbuf.tile([P, C], BF16, name="squares", tag="squares", bufs=2)
             nc.scalar.activation(out=squares[:], in_=rows, func=ACT.Square, accum_out=total)
 
         def query_norm(n):
             b, i = divmod(n, TILES)
-            if i == 0:
-                q2[b] = sbuf.tile([P, TILES], F32, name="q2", tag="q2", bufs=3)
-                z_cap[b] = sbuf.tile([P, TILES], F32, name="z_cap", tag="z_cap", bufs=3)
-            sum_of_squares(q_rows[b][:, i, :], q2[b][:, i : i + 1])
+            sum_of_squares(q_rows[b][:, i, :], q2[:, n : n + 1])
             nc.gpsimd.tensor_scalar(
-                out=z_cap[b][:, i : i + 1],
-                in0=q2[b][:, i : i + 1],
+                out=z_cap[:, n : n + 1],
+                in0=q2[:, n : n + 1],
                 scalar1=0.5 * (1.0 - D2_FLOOR_OF_Q2),
                 scalar2=-0.5 * D2_FLOOR,
                 op0=ALU.mult,
@@ -295,59 +299,55 @@ def tile_qkvattention_pa_t_kernel(tc, q_scaled, k_scaled, v, out):
 
         def cap_and_maximum(m):
             n, h = divmod(m, HALVES)
-            b, i = divmod(n, TILES)
-            if i == 0 and h == 0:
-                z_max[b] = sbuf.tile([P, TILES, HALVES], F32, name="z_max", tag="z_max", bufs=3)
             if h == 0:
-                z[n] = sbuf.tile([P, T], F32, name="z", tag="z", bufs=16, align_bytes=256)
+                z[n] = sbuf.tile([P, T], F32, name="z", tag="z", bufs=17, align_bytes=256)
             nc.vector.tensor_scalar(
                 out=z[n][:, h * BANK : (h + 1) * BANK],
                 in0=s_bank[m][:],
-                scalar1=z_cap[b][:, i : i + 1],
+                scalar1=z_cap[:, n : n + 1],
                 scalar2=None,
                 op0=ALU.min,
                 op1=ALU.max,
-                accum_out=z_max[b][:, i, h : h + 1],
+                accum_out=z_max[:, n, h : h + 1],
             )
 
-        def nearest_keys(b):
-            d2_min[b] = sbuf.tile([P, TILES], F32, name="d2_min", tag="d2_min", bufs=2)
-            nc.vector.tensor_reduce(out=d2_min[b][:], in_=z_max[b][:], axis=mybir.AxisListType.X, op=ALU.max)
+        def nearest_keys(group):
+            columns = slice(group[0], group[-1] + 1)
+            nc.vector.tensor_reduce(
+                out=d2_min[:, columns], in_=z_max[:, columns, :], axis=mybir.AxisListType.X, op=ALU.max
+            )
 
-        def nearest_distances(b):
+        def nearest_distances(group):
+            columns = slice(group[0], group[-1] + 1)
             nc.vector.scalar_tensor_tensor(
-                out=d2_min[b][:], in0=d2_min[b][:], scalar=-2.0, in1=q2[b][:], op0=ALU.mult, op1=ALU.add
+                out=d2_min[:, columns], in0=d2_min[:, columns], scalar=-2.0, in1=q2[:, columns], op0=ALU.mult, op1=ALU.add
             )
 
         def root(n):
-            b, i = divmod(n, TILES)
-            nc.scalar.activation(out=z[n][:], in_=z[n][:], func=ACT.Sqrt, scale=-2.0, bias=q2[b][:, i : i + 1])
-            if i == TILES - 1:
-                dist_min[b] = sbuf.tile([P, TILES], F32, name="dist_min", tag="dist_min", bufs=2)
-                nc.scalar.activation(out=dist_min[b][:], in_=d2_min[b][:], func=ACT.Sqrt)
+            nc.scalar.activation(out=z[n][:], in_=z[n][:], func=ACT.Sqrt, scale=-2.0, bias=q2[:, n : n + 1])
+            if n in GROUP_OF_LAST:
+                columns = slice(GROUP_OF_LAST[n][0], n + 1)
+                nc.scalar.activation(out=dist_min[:, columns], in_=d2_min[:, columns], func=ACT.Sqrt)
 
         def exp(n):
-            b, i = divmod(n, TILES)
-            if i == 0:
-                row_sum[b] = sbuf.tile([P, TILES], F32, name="row_sum", tag="row_sum", bufs=2)
             e[n] = sbuf.tile([P, T], BF16, name="e", tag="e", bufs=8, align_bytes=256)
             nc.scalar.activation(
                 out=e[n][:],
                 in_=z[n][:],
                 func=ACT.Exp,
                 scale=-1.0,
-                bias=dist_min[b][:, i : i + 1],
-                accum_out=row_sum[b][:, i : i + 1],
+                bias=dist_min[:, n : n + 1],
+                accum_out=row_sum[:, n : n + 1],
             )
 
-        def row_reciprocal(n):
-            b, i = divmod(n, TILES)
-            if i == 0:
-                row_scale[b] = sbuf.tile([P, TILES], F32, name="row_scale", tag="row_scale", bufs=2)
-            if n >= LAST_TILES:
-                nc.vector.reciprocal(out=row_scale[b][:, i : i + 1], in_=row_sum[b][:, i : i + 1])
-            elif i % PAIR == PAIR - 1:
-                nc.vector.reciprocal(out=row_scale[b][:, i - 1 : i + 1], in_=row_sum[b][:, i - 1 : i + 1])
+        def row_reciprocals(n):
+            place = n - max(group[0] for group in GROUPS if group[0] <= n)
+            first = n
+            if n < LAST_TILES and place % PAIR == 1:
+                first = n - 1
+            elif n < LAST_TILES and n not in GROUP_OF_LAST:
+                return
+            nc.vector.reciprocal(out=row_scale[:, first : n + 1], in_=row_sum[:, first : n + 1])
 
         def regroup_values(b, g):
             if g == 0:
@@ -398,12 +398,12 @@ def tile_qkvattention_pa_t_kernel(tc, q_scaled, k_scaled, v, out):
 
         def scale_and_store(n):
             b, i = divmod(n, TILES)
-            out_rows = sbuf.tile([P, C], F32, name="out_rows", tag="out_rows", bufs=4)
+            out_rows = sbuf.tile([P, C], F32, name="out_rows", tag="out_rows", bufs=6)
             if n >= SCALAR_SCALES:
-                nc.scalar.activation(out=out_rows[:], in_=acc[n][:], func=ACT.Copy, scale=row_scale[b][:, i : i + 1])
+                nc.scalar.activation(out=out_rows[:], in_=acc[n][:], func=ACT.Copy, scale=row_scale[:, n : n + 1])
             else:
                 nc.vector.tensor_scalar(
-                    out=out_rows[:], in0=acc[n][:], scalar1=row_scale[b][:, i : i + 1], scalar2=None, op0=ALU.mult
+                    out=out_rows[:], in0=acc[n][:], scalar1=row_scale[:, n : n + 1], scalar2=None, op0=ALU.mult
                 )
             nc.sync.dma_start(out=out[b, i * P : (i + 1) * P, :], in_=out_rows[:])
 
@@ -426,8 +426,8 @@ def tile_qkvattention_pa_t_kernel(tc, q_scaled, k_scaled, v, out):
                 if is_bank(m):
                     cap_and_maximum(m)
                 copy_job(step, h)
-                if h == 1 and is_tile(step) and step % TILES == TILES - 1:
-                    nearest_keys(step // TILES)
+                if h == 1 and step in GROUP_OF_LAST:
+                    nearest_keys(GROUP_OF_LAST[step])
                 if h == 0 and step < ALL_TILES and -1 < t_tile.get(step - 3, -1) < SCALAR_SCALES:
                     scale_and_store(t_tile[step - 3])
             if t_tile.get(step - 3, -1) >= SCALAR_SCALES:
@@ -439,10 +439,10 @@ def tile_qkvattention_pa_t_kernel(tc, q_scaled, k_scaled, v, out):
                     exp(todo[1])
             if done is not None:
                 quantise_e(done)
-            if is_tile(step) and step % TILES == TILES - 1:
-                nearest_distances(step // TILES)
+            if step in GROUP_OF_LAST:
+                nearest_distances(GROUP_OF_LAST[step])
             if done is not None:
-                row_reciprocal(done)
+                row_reciprocals(done)
             if t_tile.get(step - 2) is not None:
                 multiply_with_values(t_tile[step - 2])
             if step >= ALL_TILES and -1 < t_tile.get(step - 3, -1) < SCALAR_SCALES:

from contextlib import ExitStack

import concourse.mybir as mybir
from concourse.masks import make_identity

F32 = mybir.dt.float32
BF16 = mybir.dt.bfloat16
U32 = mybir.dt.uint32
U8 = mybir.dt.uint8
FP8X4 = mybir.dt.float8_e4m3fn_x4
ALU = mybir.AluOpType
ACT = mybir.ActivationFunctionType

B, T, C = 4, 1024, 512
P = 128
TILES = T // P
ALL_TILES = B * TILES
CHUNKS = C // P
BANK = 512
HALVES = T // BANK
ALL_BANKS = ALL_TILES * HALVES
TILES_PER_BANK = BANK // P
PACK = 4
PASSES = T // (P * PACK)
PAIR = 2

FLOPS = 2 * (2 * B * T * T * C)
D2_FLOOR = 2.0**-116
D2_FLOOR_OF_Q2 = 2.0**-23

FIRST_STEP = -3
GROUPS = (range(0, 11), range(11, 22), range(22, 32))
GROUP_OF_LAST = {group[-1]: group for group in GROUPS}
ROOT_LAG = 2
SCALAR_LOAD = 5
SQUARES_AHEAD = 8
QUERY_AHEAD = 2
KEYS_DUE = 6
VALUES_AHEAD = 7
QUANTISE_LAG = 3
SCALAR_SCALES = 24
LAST_TILES = 26
VECTOR_SQUARES = 2


def squared_by_vector(b, j):
    return b < B - 1 and j % VECTOR_SQUARES == VECTOR_SQUARES - 1


def scalar_plan():
    squares = [(FIRST_STEP, ("k", 0, j)) for j in range(TILES_PER_BANK)]
    squares += [(FIRST_STEP + 1, ("q", 0))]
    squares += [(FIRST_STEP + 2, ("k", 0, j)) for j in range(TILES_PER_BANK, TILES)]
    rest = [(n - 2, ("q", n)) for n in range(1, ALL_TILES)]
    rest += [(TILES * b - KEYS_DUE + j // 4, ("k", b, j)) for b in range(1, B) for j in range(TILES)]
    squares += sorted(rest, key=lambda item: item[0])
    passes = []
    for group in GROUPS:
        passes += [("root", n) for n in group]
        passes += [("exp", n) for n in group]

    def load_of(item):
        return 0 if item[0] == "k" and squared_by_vector(item[1], item[2]) else 1

    plan = {}
    step = FIRST_STEP
    s = 0
    a = 0
    while s < len(squares) or a < len(passes):
        plan[step] = []
        load = 0
        while s < len(squares) and squares[s][0] <= step:
            plan[step] += [squares[s][1]]
            load += load_of(squares[s][1])
            s += 1
        while a < len(passes) and load + 2 <= SCALAR_LOAD and (passes[a][0] == "exp" or passes[a][1] <= step - ROOT_LAG):
            plan[step] += [passes[a]]
            load += 2
            a += 1
        while s < len(squares) and load < SCALAR_LOAD and squares[s][0] <= step + SQUARES_AHEAD:
            plan[step] += [squares[s][1]]
            load += load_of(squares[s][1])
            s += 1
        step += 1
    return plan


def transpose_steps(plan):
    steps = {}
    for step, items in plan.items():
        for item in items:
            if item[0] == "exp":
                steps[item[1]] = max(step + 1, steps.get(item[1] - 1, step) + 1)
    return steps


def transpose_plan(steps):
    plan = {
        (FIRST_STEP, 0): ("k", 0, 0),
        (FIRST_STEP, 1): ("k", 0, 1),
        (FIRST_STEP + 1, 0): ("q", 0),
        (FIRST_STEP + 1, 1): ("k", 0, 2),
        (FIRST_STEP + 2, 0): ("k", 0, 3),
    }
    for n in range(PAIR, ALL_TILES, PAIR):
        plan[n - QUERY_AHEAD, 0] = ("q", n // PAIR)
    for n, step in steps.items():
        plan[step, 1] = ("e", n)
    half = 1
    for b in range(1, B):
        for pair in range(TILES // PAIR):
            while divmod(half, HALVES) in plan:
                half += 1
            plan[divmod(half, HALVES)] = ("k", b, pair)
    return plan


def tile_qkvattention_pa_t_kernel(tc, q_scaled, k_scaled, v, out):
    nc = tc.nc
    with ExitStack() as stack:
        sbuf = stack.enter_context(tc.tile_pool(name="sbuf", bufs=1))
        psum = stack.enter_context(tc.psum_pool(name="psum", bufs=1))
        stack.enter_context(tc.manual_schedule())

        plan = scalar_plan()
        t_step = transpose_steps(plan)
        t_tile = {step: n for n, step in t_step.items()}
        jobs = transpose_plan(t_step)
        last_step = t_step[ALL_TILES - 1] + 3

        identity = sbuf.tile([P, P], F32, name="identity", align_bytes=256)
        make_identity(nc, identity[:])

        q_rows, k_rows, v_rows = {}, {}, {}
        k2, bank_start, k_t = {}, {}, {}
        q2 = sbuf.tile([P, ALL_TILES], F32, name="q2")
        z_cap = sbuf.tile([P, ALL_TILES], F32, name="z_cap")
        z_max = sbuf.tile([P, ALL_TILES, HALVES], F32, name="z_max")
        d2_min = sbuf.tile([P, ALL_TILES], F32, name="d2_min")
        dist_min = sbuf.tile([P, ALL_TILES], F32, name="dist_min")
        row_sum = sbuf.tile([P, ALL_TILES], F32, name="row_sum")
        row_scale = sbuf.tile([P, ALL_TILES], F32, name="row_scale")
        v_grouped, v_codes, v_scales = {}, {}, {}
        q_t, z, e, e_grouped, e_codes, e_scales, acc = {}, {}, {}, {}, {}, {}, {}
        s_bank, t_bank = {}, {}

        def is_tile(n):
            return 0 <= n < ALL_TILES

        def is_bank(m):
            return 0 <= m < ALL_BANKS

        def load_keys(b, first, last):
            if first == 0:
                k_rows[b] = sbuf.tile([P, TILES, C], BF16, name="k_rows", tag="k_rows", bufs=B, align_bytes=256)
            source = k_scaled[b].rearrange("(i p) c -> p i c", p=P)
            nc.sync.dma_start(out=k_rows[b][:, first:last, :], in_=source[:, first:last, :])

        def load_queries(b, first, last):
            if first == 0:
                q_rows[b] = sbuf.tile([P, TILES, C], BF16, name="q_rows", tag="q_rows", bufs=2, align_bytes=256)
            source = q_scaled[b].rearrange("(i p) c -> p i c", p=P)
            nc.sync.dma_start(out=q_rows[b][:, first:last, :], in_=source[:, first:last, :])

        def load_values(b):
            v_rows[b] = sbuf.tile([P, PASSES, PACK, C], BF16, name="v_rows", tag="v_rows", bufs=2)
            nc.sync.dma_start(
                out=v_rows[b][:].rearrange("p g (u w) c -> p (g u) (w c)", w=PAIR),
                in_=v[b].rearrange("(a p w) c -> p a (w c)", p=P, w=PAIR),
            )

        def load_inputs(step):
            if step == FIRST_STEP:
                load_keys(0, 0, 2)
                load_keys(0, 2, 4)
                load_queries(0, 0, 2)
                load_keys(0, 4, 6)
                load_keys(0, 6, 8)
                load_queries(0, 2, 8)
                load_keys(1, 0, 8)
                load_values(0)
                load_queries(1, 0, 8)
                load_keys(2, 0, 8)
                load_keys(3, 0, 8)
                load_values(1)
            for b in (2, 3):
                if step == TILES * (b - 1) - 3:
                    load_queries(b, 0, 8)
                if step == t_step[TILES * (b - 2)] + 1:
                    load_values(b)

        def sum_of_squares(rows, total, vec=False):
            if vec:
                squares = sbuf.tile([P, C], F32, name="squares2", tag="squares2", bufs=2)
                nc.vector.scalar_tensor_tensor(
                    out=squares[:], in0=rows, scalar=1.0, in1=rows, op0=ALU.mult, op1=ALU.mult, accum_out=total
                )
                return
            squares = sbuf.tile([P, C], BF16, name="squares", tag="squares", bufs=2)
            nc.scalar.activation(out=squares[:], in_=rows, func=ACT.Square, accum_out=total)

        def query_norm(n):
            b, i = divmod(n, TILES)
            sum_of_squares(q_rows[b][:, i, :], q2[:, n : n + 1])
            nc.gpsimd.tensor_scalar(
                out=z_cap[:, n : n + 1],
                in0=q2[:, n : n + 1],
                scalar1=0.5 * (1.0 - D2_FLOOR_OF_Q2),
                scalar2=-0.5 * D2_FLOOR,
                op0=ALU.mult,
                op1=ALU.add,
            )

        def key_norm(b, j):
            if b not in k2:
                k2[b] = sbuf.tile([P, TILES], F32, name="k2", tag="k2", bufs=3)
                bank_start[b] = sbuf.tile([P, TILES], F32, name="bank_start", tag="bank_start", bufs=4)
            sum_of_squares(k_rows[b][:, j, :], k2[b][:, j : j + 1], squared_by_vector(b, j))
            nc.gpsimd.tensor_scalar(
                out=bank_start[b][:, j : j + 1],
                in0=k2[b][:, j : j + 1],
                scalar1=-0.5,
                scalar2=0.0,
                op0=ALU.mult,
                op1=ALU.add,
            )

        def transpose_part(step, h, r):
            job = jobs.get((step, h))
            if job is None:
                return
            if r == 0:
                t_bank[step, h] = psum.tile([P, PAIR, PAIR, P], F32, name="t_bank", tag="transposes", bufs=3)
            a, u = divmod(r, PAIR)
            words = slice(u * P, (u + 1) * P)
            if job[0] == "q":
                b, i = divmod(PAIR * job[1] + a, TILES)
                source = q_rows[b][:, i, :].bitcast(F32)[:, words]
            elif job[0] == "k":
                source = k_rows[job[1]][:, PAIR * job[2] + a, :].bitcast(F32)[:, words]
            else:
                source = e[job[1]][:].bitcast(F32)[:, r * P : (r + 1) * P]
            nc.tensor.transpose(out=t_bank[step, h][:, a, u, :], in_=source, identity=identity[:])

        def copy_job(step, h):
            job = jobs.get((step, h))
            if job is None:
                return
            bank = t_bank[step, h]
            if job[0] == "q":
                pair = sbuf.tile([P, PAIR, PAIR, P], F32, name="q_t", tag="q_t", bufs=3, align_bytes=256)
                nc.vector.tensor_copy(out=pair[:], in_=bank[:])
                for a in range(PAIR):
                    q_t[PAIR * job[1] + a] = pair[:, a]
            elif job[0] == "k":
                b, j = job[1], job[2]
                if j == 0:
                    k_t[b] = sbuf.tile([P, PAIR, T], F32, name="k_t", tag="k_t", bufs=B, align_bytes=256)
                for i in range(PAIR * j, PAIR * (j + 1)):
                    if b > 0 and squared_by_vector(b, i):
                        key_norm(b, i)
                cols = slice(j * PAIR * P, (j + 1) * PAIR * P)
                nc.vector.tensor_copy(
                    out=k_t[b][:, :, cols].rearrange("p u (a s) -> p u a s", a=PAIR), in_=bank[:].rearrange("p a u s -> p u a s")
                )
            else:
                n = job[1]
                e_grouped[n] = sbuf.tile(
                    [P, PASSES, P, PACK], BF16, name="e_grouped", tag="e_grouped", bufs=3, align_bytes=256
                )
                nc.vector.tensor_copy(out=e_grouped[n][:].bitcast(F32), in_=bank[:].rearrange("p g u t -> p g t u"))

        def start_bank(m, r):
            n, h = divmod(m, HALVES)
            if r == 0:
                s_bank[m] = psum.tile([P, BANK], F32, name="s_bank", tag="s_bank", bufs=3)
            j = TILES_PER_BANK * h + r
            nc.tensor.matmul(
                out=s_bank[m][:, r * P : (r + 1) * P],
                lhsT=bank_start[n // TILES][:, j : j + 1].to_broadcast([P, P]),
                rhs=identity[:],
                start=(r == 0),
                stop=False,
                is_transpose=True,
            )

        def score_matmul(m, c):
            n, h = divmod(m, HALVES)
            u, w = divmod(c, PAIR)
            queries = q_t[n].bitcast(BF16).rearrange("p u (t w) -> p u t w", w=PAIR)
            keys = k_t[n // TILES][:].bitcast(BF16).rearrange("p u (s w) -> p u s w", w=PAIR)
            nc.tensor.matmul(
                out=s_bank[m][:],
                lhsT=queries[:, u, :, w],
                rhs=keys[:, u, h * BANK : (h + 1) * BANK, w],
                start=False,
                stop=(c == CHUNKS - 1),
            )

        def cap_and_maximum(m):
            n, h = divmod(m, HALVES)
            if h == 0:
                z[n] = sbuf.tile([P, T], F32, name="z", tag="z", bufs=17, align_bytes=256)
            nc.vector.tensor_scalar(
                out=z[n][:, h * BANK : (h + 1) * BANK],
                in0=s_bank[m][:],
                scalar1=z_cap[:, n : n + 1],
                scalar2=None,
                op0=ALU.min,
                op1=ALU.max,
                accum_out=z_max[:, n, h : h + 1],
            )

        def nearest_keys(group):
            columns = slice(group[0], group[-1] + 1)
            nc.vector.tensor_reduce(
                out=d2_min[:, columns], in_=z_max[:, columns, :], axis=mybir.AxisListType.X, op=ALU.max
            )

        def nearest_distances(group):
            columns = slice(group[0], group[-1] + 1)
            nc.vector.scalar_tensor_tensor(
                out=d2_min[:, columns], in0=d2_min[:, columns], scalar=-2.0, in1=q2[:, columns], op0=ALU.mult, op1=ALU.add
            )

        def root(n):
            nc.scalar.activation(out=z[n][:], in_=z[n][:], func=ACT.Sqrt, scale=-2.0, bias=q2[:, n : n + 1])
            if n in GROUP_OF_LAST:
                columns = slice(GROUP_OF_LAST[n][0], n + 1)
                nc.scalar.activation(out=dist_min[:, columns], in_=d2_min[:, columns], func=ACT.Sqrt)

        def exp(n):
            e[n] = sbuf.tile([P, T], BF16, name="e", tag="e", bufs=8, align_bytes=256)
            nc.scalar.activation(
                out=e[n][:],
                in_=z[n][:],
                func=ACT.Exp,
                scale=-1.0,
                bias=dist_min[:, n : n + 1],
                accum_out=row_sum[:, n : n + 1],
            )

        def row_reciprocals(n):
            place = n - max(group[0] for group in GROUPS if group[0] <= n)
            first = n
            if n < LAST_TILES and place % PAIR == 1:
                first = n - 1
            elif n < LAST_TILES and n not in GROUP_OF_LAST:
                return
            nc.vector.reciprocal(out=row_scale[:, first : n + 1], in_=row_sum[:, first : n + 1])

        def regroup_values(b, g):
            if g == 0:
                v_codes[b] = sbuf.tile([P, PASSES, C], U32, name="v_codes", tag="v_codes", bufs=2, align_bytes=256)
                v_scales[b] = sbuf.tile([P, PASSES, C], U8, name="v_scales", tag="v_scales", bufs=2, align_bytes=256)
            v_grouped[b, g] = sbuf.tile([P, C, PACK], BF16, name="v_grouped", tag="v_grouped", bufs=2, align_bytes=256)
            nc.gpsimd.tensor_scalar(
                out=v_grouped[b, g][:].rearrange("p (c r) j -> p c j r", r=4),
                in0=v_rows[b][:, g].rearrange("p j (c r) -> p c j r", r=4),
                scalar1=1.0,
                scalar2=0.0,
                op0=ALU.mult,
                op1=ALU.add,
            )

        def quantise_values(b, g):
            nc.vector.quantize_mx(
                out=v_codes[b][:, g, :].bitcast(FP8X4),
                scales=v_scales[b][:, g, :],
                in_=v_grouped[b, g][:].rearrange("p c j -> p (c j)"),
            )

        def quantise_e(n):
            e_codes[n] = sbuf.tile([P, PASSES, P], U32, name="e_codes", tag="e_codes", bufs=3, align_bytes=256)
            e_scales[n] = sbuf.tile([P, PASSES, P], U8, name="e_scales", tag="e_scales", bufs=3, align_bytes=256)
            nc.vector.quantize_mx(
                out=e_codes[n][:].rearrange("p g t -> p (g t)").bitcast(FP8X4),
                scales=e_scales[n][:].rearrange("p g t -> p (g t)"),
                in_=e_grouped[n][:].rearrange("p g t j -> p (g t j)"),
            )

        def multiply_with_values(n):
            b = n // TILES
            if n < LAST_TILES:
                acc[n] = psum.tile([P, C], F32, name="acc", tag="acc", bufs=2)
            else:
                acc[n] = psum.tile([P, C], F32, name="acc", tag="s_bank", bufs=3)
            for g in range(PASSES):
                nc.tensor.matmul_mx(
                    out=acc[n][:],
                    lhsT=e_codes[n][:, g, :].bitcast(FP8X4),
                    lhsT_scale=e_scales[n][:, g, :],
                    rhs=v_codes[b][:, g, :].bitcast(FP8X4),
                    rhs_scale=v_scales[b][:, g, :],
                    start=(g == 0),
                    stop=(g == PASSES - 1),
                )

        def scale_and_store(n):
            b, i = divmod(n, TILES)
            out_rows = sbuf.tile([P, C], F32, name="out_rows", tag="out_rows", bufs=6)
            if n >= SCALAR_SCALES:
                nc.scalar.activation(out=out_rows[:], in_=acc[n][:], func=ACT.Copy, scale=row_scale[:, n : n + 1])
            else:
                nc.vector.tensor_scalar(
                    out=out_rows[:], in0=acc[n][:], scalar1=row_scale[:, n : n + 1], scalar2=None, op0=ALU.mult
                )
            nc.sync.dma_start(out=out[b, i * P : (i + 1) * P, :], in_=out_rows[:])

        for step in range(FIRST_STEP, last_step + 1):
            load_inputs(step)
            for todo in plan.get(step, []):
                if todo[0] == "k" and not (todo[1] > 0 and squared_by_vector(todo[1], todo[2])):
                    key_norm(todo[1], todo[2])
                elif todo[0] == "q":
                    query_norm(todo[1])
            done = t_tile.get(step - 1)
            for h in range(HALVES):
                m = HALVES * step + h
                for c in range(CHUNKS):
                    if is_bank(m):
                        score_matmul(m, c)
                    if is_bank(m + 1):
                        start_bank(m + 1, c)
                    transpose_part(step, h, c)
                if is_bank(m):
                    cap_and_maximum(m)
                copy_job(step, h)
                if h == 1 and step in GROUP_OF_LAST:
                    nearest_keys(GROUP_OF_LAST[step])
                if h == 0 and step < ALL_TILES and -1 < t_tile.get(step - 3, -1) < SCALAR_SCALES:
                    scale_and_store(t_tile[step - 3])
            if t_tile.get(step - 3, -1) >= SCALAR_SCALES:
                scale_and_store(t_tile[step - 3])
            for todo in plan.get(step, []):
                if todo[0] == "root":
                    root(todo[1])
                elif todo[0] == "exp":
                    exp(todo[1])
            if done is not None:
                quantise_e(done)
            if step in GROUP_OF_LAST:
                nearest_distances(GROUP_OF_LAST[step])
            if done is not None:
                row_reciprocals(done)
            if t_tile.get(step - 2) is not None:
                multiply_with_values(t_tile[step - 2])
            if step >= ALL_TILES and -1 < t_tile.get(step - 3, -1) < SCALAR_SCALES:
                scale_and_store(t_tile[step - 3])
            for b in range(B):
                for g in range(PASSES):
                    if step == t_step[TILES * b] - VALUES_AHEAD + 2 * g:
                        regroup_values(b, g)
                    if step == t_step[TILES * b] - VALUES_AHEAD + QUANTISE_LAG + 2 * g:
                        quantise_values(b, g)
